import numpy as np
import ml_dtypes


def mxq(x, axis, fmt="e4m3"):
    dtype, down = {"e4m3": (ml_dtypes.float8_e4m3fn, 7), "e5m2": (ml_dtypes.float8_e5m2, 14)}[fmt]
    v = np.moveaxis(np.asarray(x, np.float32).astype(ml_dtypes.bfloat16).astype(np.float64), axis, -1)
    blocks = v.reshape(v.shape[:-1] + (-1, 32))
    amax = np.abs(blocks).max(-1, keepdims=True)
    byte = np.maximum(np.where(amax > 0, np.frexp(amax)[1] - 1 + 127, 0) - down, 1)
    scale = np.exp2(byte - 127.0)
    codes = (blocks / scale).astype(np.float32).astype(dtype).astype(np.float64)
    return np.moveaxis((codes * scale).reshape(v.shape), -1, axis)


WIDE = False


def mx_kscale(k):
    if not WIDE:
        return np.ones(k)
    levels = np.array([10, -10, 5, -5, 0])
    a = np.random.permutation(np.resize(levels, k // 512 * 4)).reshape(k // 512, 4)
    idx = np.arange(k)
    return np.exp2(a[idx // 512, idx % 128 // 32])


BF16 = ml_dtypes.bfloat16


def bf(x):
    return np.asarray(x, np.float32).astype(BF16)


def f64(x):
    return np.asarray(x).astype(np.float64)


B, S, HID, NH, DH = 4, 256, 1024, 16, 64
DQ = NH * DH


def setup_inputs():
    s = mx_kscale(DQ)
    y = np.random.standard_normal((B, S, DQ)) * 0.3 * s
    h = np.ascontiguousarray(y.reshape(B, NH, S, DH).transpose(0, 2, 1, 3))
    return {"h_attn": bf(h),
            "Wo": bf(np.random.standard_normal((DQ, HID)) * 1.5 / np.sqrt(DQ) / s[:, None]),
            "bo": bf(np.random.standard_normal(HID) * 0.3)}


def reference(h_attn, Wo, bo):
    y = f64(h_attn).transpose(0, 2, 1, 3).reshape(B, -1, DQ)
    return (mxq(y, 2, "e4m3") @ mxq(f64(Wo), 0, "e4m3")) + f64(bo)

@@ -1,0 +1,168 @@
+from contextlib import ExitStack
+
+from concourse import mybir
+from concourse.masks import make_identity
+
+BF16 = mybir.dt.bfloat16
+F32 = mybir.dt.float32
+U32 = mybir.dt.uint32
+U8 = mybir.dt.uint8
+FP8X4 = mybir.dt.float8_e4m3fn_x4
+
+P = 128
+BATCH, TOKENS, HEADS, DH = 4, 256, 16, 64
+K = HEADS * DH
+N = 1024
+K_PASS = 4 * P
+PASSES = K // K_PASS
+N_HALF = 512
+HEAD_HALVES = 2
+HEADS_ROUND = HEADS // HEAD_HALVES
+TOK_PASS = 8
+WORDS_HEAD = TOK_PASS * DH // 2
+
+FLOPS = 2 * BATCH * TOKENS * K * N
+
+
+def tile_reasoningmultiheadattention_pb_kernel(tc, h_attn, Wo, bo, out):
+    nc = tc.nc
+    with ExitStack() as stack:
+        const = stack.enter_context(tc.tile_pool(name="const", bufs=1))
+        keep = stack.enter_context(tc.tile_pool(name="keep", bufs=1))
+        rounds = stack.enter_context(tc.tile_pool(name="rounds", bufs=2))
+        wstage = stack.enter_context(tc.tile_pool(name="wstage", bufs=4))
+        results = stack.enter_context(tc.tile_pool(name="results", bufs=8))
+        tpsum = stack.enter_context(tc.psum_pool(name="tpsum", bufs=4))
+        acc_psum = stack.enter_context(tc.psum_pool(name="acc_psum", bufs=4))
+
+        h_view = h_attn.rearrange(
+            "b (tg jp) (hh hl) d -> (b tg) jp hh (hl d)", jp=TOK_PASS, hh=HEAD_HALVES
+        )
+        w_view = Wo.rearrange("(g u p e) n -> g u p e n", g=PASSES, u=2, e=2)
+        out_rows = out.flatten_outer_dims()
+
+        bias_row = const.tile([P, N], BF16)
+        nc.vector.memset(bias_row[:], 0.0)
+
+        w_raw = []
+        x_raw = []
+
+        def load_w(nh):
+            raw = keep.tile([P, PASSES, 4, N_HALF], BF16, name="w_raw%d" % nh)
+            for g in range(PASSES):
+                for u in range(2):
+                    nc.sync.dma_start(
+                        out=raw[:, g, 2 * u : 2 * u + 2, :],
+                        in_=w_view[g, u][:, :, nh * N_HALF : (nh + 1) * N_HALF],
+                    )
+                if nh == 0 and g == 0:
+                    nc.sync.dma_start(out=bias_row[0:1, :], in_=bo.unsqueeze(0))
+            w_raw.append(raw)
+
+        def load_x(hh):
+            raw = keep.tile([P, TOK_PASS, HEADS_ROUND * DH], BF16, name="x_raw%d" % hh)
+            nc.sync.dma_start(out=raw[:], in_=h_view[:, :, hh, :])
+            x_raw.append(raw)
+
+        load_w(0)
+        load_x(0)
+        load_x(1)
+        load_w(1)
+
+        ident = const.tile([P, P], F32)
+        make_identity(nc, ident[:])
+        perm = const.tile([P, P], F32)
+        nc.vector.tensor_copy(
+            out=perm[:].rearrange("p (b g thi) -> p b g thi", b=BATCH, g=PASSES),
+            in_=ident[:].rearrange("p (b thi g) -> p b g thi", b=BATCH, g=PASSES),
+        )
+        ones = const.tile([P, P], BF16)
+        nc.vector.memset(ones[:], 1.0)
+
+        bias = const.tile([P, N], F32)
+        for nh in range(2):
+            cols = slice(nh * N_HALF, (nh + 1) * N_HALF)
+            spread = acc_psum.tile([P, N_HALF], F32, name="acc")
+            nc.tensor.matmul(out=spread[:], lhsT=ones[:], rhs=bias_row[:, cols], start=True, stop=True)
+            nc.vector.tensor_copy(out=bias[:, cols], in_=spread[:])
+
+        w_codes = keep.tile([P, PASSES, N], U32, align_bytes=64)
+        w_scales = keep.tile([P, PASSES, N], U8, align_bytes=64)
+        y_codes = keep.tile([P, HEAD_HALVES * BATCH * PASSES * P], U32, align_bytes=64)
+        y_scales = keep.tile([P, HEAD_HALVES * BATCH * PASSES * P], U8, align_bytes=64)
+
+        def quantise_w(nh):
+            cols = slice(nh * N_HALF, (nh + 1) * N_HALF)
+            for g in range(PASSES):
+                grouped = wstage.tile([P, N_HALF, 4], BF16, align_bytes=64, name="w_grouped")
+                nc.scalar.copy(
+                    out=grouped[:].rearrange("p (c i) t -> p c t i", i=4),
+                    in_=w_raw[nh][:, g].rearrange("p t (c i) -> p c t i", i=4),
+                )
+                nc.vector.quantize_mx(
+                    out=w_codes[:, g, cols].bitcast(FP8X4),
+                    scales=w_scales[:, g, cols],
+                    in_=grouped[:].rearrange("p n t -> p (n t)"),
+                )
+
+        def quantise_y(hh):
+            by_head = rounds.tile([P, HEADS_ROUND * TOK_PASS * DH], BF16, name="by_head")
+            grouped = rounds.tile([P, BATCH * PASSES * P * 4], BF16, align_bytes=64, name="y_grouped")
+            by_head_words = by_head[:].bitcast(F32)
+            grouped_words = grouped[:].bitcast(F32).rearrange(
+                "p (bg q m u) -> p q bg m u", bg=BATCH * PASSES, q=4, u=2
+            )
+            for q in range(4):
+                heads = slice(2 * q, 2 * q + 2)
+                nc.vector.tensor_copy(
+                    out=by_head[:].rearrange("p (hl jp d) -> p hl jp d", hl=HEADS_ROUND, jp=TOK_PASS)[:, heads],
+                    in_=x_raw[hh][:].rearrange("p jp (hl d) -> p hl jp d", d=DH)[:, heads],
+                )
+                bank = tpsum.tile([P, 512], F32, name="bank")
+                bank_out = bank[:].rearrange("p (u bg hlo thi) -> p u bg hlo thi", u=2, bg=BATCH * PASSES, hlo=2)
+                for hlo in range(2):
+                    for u in range(2):
+                        first = ((2 * q + hlo) * 2 + u) * P
+                        nc.tensor.transpose(
+                            bank_out[:, u, :, hlo, :], by_head_words[:, first : first + P], perm[:]
+                        )
+                nc.scalar.copy(
+                    out=grouped_words[:, q],
+                    in_=bank[:].rearrange("p (u bg m) -> p bg m u", u=2, bg=BATCH * PASSES),
+                )
+            for b in range(BATCH):
+                words = slice((hh * BATCH + b) * PASSES * P, (hh * BATCH + b + 1) * PASSES * P)
+                nc.vector.quantize_mx(
+                    out=y_codes[:, words].bitcast(FP8X4),
+                    scales=y_scales[:, words],
+                    in_=grouped[:, b * PASSES * P * 4 : (b + 1) * PASSES * P * 4],
+                )
+
+        def multiply(hh, nh):
+            cols = slice(nh * N_HALF, (nh + 1) * N_HALF)
+            for b in range(BATCH):
+                acc = acc_psum.tile([P, N_HALF], F32, name="acc")
+                for g in range(PASSES):
+                    first = ((hh * BATCH + b) * PASSES + g) * P
+                    nc.tensor.matmul_mx(
+                        out=acc[:],
+                        lhsT=y_codes[:, first : first + P].bitcast(FP8X4),
+                        lhsT_scale=y_scales[:, first : first + P],
+                        rhs=w_codes[:, g, cols].bitcast(FP8X4),
+                        rhs_scale=w_scales[:, g, cols],
+                        start=(g == 0),
+                        stop=(g == PASSES - 1),
+                    )
+                result = results.tile([P, N_HALF], F32, name="result")
+                nc.vector.tensor_tensor(out=result[:], in0=acc[:], in1=bias[:, cols], op=mybir.AluOpType.add)
+                row = (b * HEAD_HALVES + hh) * P
+                nc.sync.dma_start(out=out_rows[row : row + P, cols], in_=result[:])
+
+        quantise_w(0)
+        quantise_y(0)
+        multiply(0, 0)
+        quantise_y(1)
+        multiply(1, 0)
+        quantise_w(1)
+        multiply(0, 1)
+        multiply(1, 1)

@@ -8,18 +8,22 @@ F32 = mybir.dt.float32
 U32 = mybir.dt.uint32
 U8 = mybir.dt.uint8
 FP8X4 = mybir.dt.float8_e4m3fn_x4
+ADD = mybir.AluOpType.add
 
 P = 128
 BATCH, TOKENS, HEADS, DH = 4, 256, 16, 64
 K = HEADS * DH
 N = 1024
-K_PASS = 4 * P
-PASSES = K // K_PASS
+PACK = 4
+PASSES = K // (PACK * P)
 N_HALF = 512
-HEAD_HALVES = 2
-HEADS_ROUND = HEADS // HEAD_HALVES
+ROUNDS = 2
+HEADS_ROUND = HEADS // ROUNDS
 TOK_PASS = 8
-WORDS_HEAD = TOK_PASS * DH // 2
+DW = DH // 2
+BANK_HEADS = 2
+BANKS_ROUND = HEADS_ROUND // BANK_HEADS
+TILE_WORDS = PASSES * P
 
 FLOPS = 2 * BATCH * TOKENS * K * N
 
@@ -29,140 +33,177 @@ def tile_reasoningmultiheadattention_pb_kernel(tc, h_attn, Wo, bo, out):
     with ExitStack() as stack:
         const = stack.enter_context(tc.tile_pool(name="const", bufs=1))
         keep = stack.enter_context(tc.tile_pool(name="keep", bufs=1))
-        rounds = stack.enter_context(tc.tile_pool(name="rounds", bufs=2))
         wstage = stack.enter_context(tc.tile_pool(name="wstage", bufs=4))
         results = stack.enter_context(tc.tile_pool(name="results", bufs=8))
-        tpsum = stack.enter_context(tc.psum_pool(name="tpsum", bufs=4))
-        acc_psum = stack.enter_context(tc.psum_pool(name="acc_psum", bufs=4))
+        psum = stack.enter_context(tc.psum_pool(name="psum", bufs=8))
+        stack.enter_context(tc.manual_schedule())
 
         h_view = h_attn.rearrange(
-            "b (tg jp) (hh hl) d -> (b tg) jp hh (hl d)", jp=TOK_PASS, hh=HEAD_HALVES
+            "b (tg jp) (r hl) d -> (b tg) jp r (hl d)", jp=TOK_PASS, r=ROUNDS
         )
         w_view = Wo.rearrange("(g u p e) n -> g u p e n", g=PASSES, u=2, e=2)
         out_rows = out.flatten_outer_dims()
 
         bias_row = const.tile([P, N], BF16)
-        nc.vector.memset(bias_row[:], 0.0)
-
-        w_raw = []
-        x_raw = []
-
-        def load_w(nh):
-            raw = keep.tile([P, PASSES, 4, N_HALF], BF16, name="w_raw%d" % nh)
-            for g in range(PASSES):
-                for u in range(2):
-                    nc.sync.dma_start(
-                        out=raw[:, g, 2 * u : 2 * u + 2, :],
-                        in_=w_view[g, u][:, :, nh * N_HALF : (nh + 1) * N_HALF],
-                    )
-                if nh == 0 and g == 0:
-                    nc.sync.dma_start(out=bias_row[0:1, :], in_=bo.unsqueeze(0))
-            w_raw.append(raw)
-
-        def load_x(hh):
-            raw = keep.tile([P, TOK_PASS, HEADS_ROUND * DH], BF16, name="x_raw%d" % hh)
-            nc.sync.dma_start(out=raw[:], in_=h_view[:, :, hh, :])
-            x_raw.append(raw)
-
-        load_w(0)
-        load_x(0)
-        load_x(1)
-        load_w(1)
-
+        ones = const.tile([P, P], BF16)
+        warm = const.tile([P, 1], BF16)
         ident = const.tile([P, P], F32)
-        make_identity(nc, ident[:])
         perm = const.tile([P, P], F32)
+        bias = const.tile([P, N], F32)
+        w_raw = keep.tile([P, 2, PASSES, PACK, N_HALF], BF16)
+        x_raw = keep.tile([P, ROUNDS, TOK_PASS, HEADS_ROUND * DH], BF16)
+        by_head = keep.tile([P, ROUNDS, HEADS_ROUND * TOK_PASS * DH], BF16)
+        y_grouped = keep.tile([P, ROUNDS, BATCH * TILE_WORDS * PACK], BF16, align_bytes=64)
+        w_codes = keep.tile([P, PASSES, N], U32, align_bytes=64)
+        w_scales = keep.tile([P, PASSES, N], U8, align_bytes=64)
+        y_codes = keep.tile([P, ROUNDS, BATCH, TILE_WORDS], U32, align_bytes=64)
+        y_scales = keep.tile([P, ROUNDS, BATCH, TILE_WORDS], U8, align_bytes=64)
+
+        def half(nh):
+            return slice(nh * N_HALF, (nh + 1) * N_HALF)
+
+        def load_w(nh, g):
+            for u in range(2):
+                nc.sync.dma_start(
+                    out=w_raw[:, nh, g, 2 * u : 2 * u + 2, :], in_=w_view[g, u][:, :, half(nh)]
+                )
+
+        def load_x(r):
+            nc.sync.dma_start(out=x_raw[:, r], in_=h_view[:, :, r, :])
+
+        nc.vector.memset(bias_row[:], 0.0)
+        nc.vector.memset(ones[:], 1.0)
+        nc.scalar.copy(out=warm[:], in_=ones[:, 0:1])
+        load_x(0)
+        nc.sync.dma_start(out=bias_row[0:1, :], in_=bo.unsqueeze(0))
+        load_w(0, 0)
+        load_w(0, 1)
+        load_x(1)
+        load_w(1, 0)
+        load_w(1, 1)
+
+        make_identity(nc, ident[:])
         nc.vector.tensor_copy(
             out=perm[:].rearrange("p (b g thi) -> p b g thi", b=BATCH, g=PASSES),
             in_=ident[:].rearrange("p (b thi g) -> p b g thi", b=BATCH, g=PASSES),
         )
-        ones = const.tile([P, P], BF16)
-        nc.vector.memset(ones[:], 1.0)
 
-        bias = const.tile([P, N], F32)
-        for nh in range(2):
-            cols = slice(nh * N_HALF, (nh + 1) * N_HALF)
-            spread = acc_psum.tile([P, N_HALF], F32, name="acc")
-            nc.tensor.matmul(out=spread[:], lhsT=ones[:], rhs=bias_row[:, cols], start=True, stop=True)
-            nc.vector.tensor_copy(out=bias[:, cols], in_=spread[:])
-
-        w_codes = keep.tile([P, PASSES, N], U32, align_bytes=64)
-        w_scales = keep.tile([P, PASSES, N], U8, align_bytes=64)
-        y_codes = keep.tile([P, HEAD_HALVES * BATCH * PASSES * P], U32, align_bytes=64)
-        y_scales = keep.tile([P, HEAD_HALVES * BATCH * PASSES * P], U8, align_bytes=64)
-
-        def quantise_w(nh):
-            cols = slice(nh * N_HALF, (nh + 1) * N_HALF)
-            for g in range(PASSES):
-                grouped = wstage.tile([P, N_HALF, 4], BF16, align_bytes=64, name="w_grouped")
-                nc.scalar.copy(
-                    out=grouped[:].rearrange("p (c i) t -> p c t i", i=4),
-                    in_=w_raw[nh][:, g].rearrange("p t (c i) -> p c t i", i=4),
+        def spread_bias():
+            for nh in range(2):
+                spread = psum.tile([P, N_HALF], F32, name="bank")
+                nc.tensor.matmul(
+                    out=spread[:], lhsT=ones[:], rhs=bias_row[:, half(nh)], start=True, stop=True
                 )
-                nc.vector.quantize_mx(
-                    out=w_codes[:, g, cols].bitcast(FP8X4),
-                    scales=w_scales[:, g, cols],
-                    in_=grouped[:].rearrange("p n t -> p (n t)"),
-                )
+                nc.vector.tensor_copy(out=bias[:, half(nh)], in_=spread[:])
 
-        def quantise_y(hh):
-            by_head = rounds.tile([P, HEADS_ROUND * TOK_PASS * DH], BF16, name="by_head")
-            grouped = rounds.tile([P, BATCH * PASSES * P * 4], BF16, align_bytes=64, name="y_grouped")
-            by_head_words = by_head[:].bitcast(F32)
-            grouped_words = grouped[:].bitcast(F32).rearrange(
-                "p (bg q m u) -> p q bg m u", bg=BATCH * PASSES, q=4, u=2
+        def regroup_w(nh, g, copy):
+            grouped = wstage.tile([P, N_HALF, PACK], BF16, align_bytes=64, name="w_grouped")
+            copy(
+                out=grouped[:].rearrange("p (c i) t -> p c t i", i=4),
+                in_=w_raw[:, nh, g].rearrange("p t (c i) -> p c t i", i=4),
             )
-            for q in range(4):
-                heads = slice(2 * q, 2 * q + 2)
-                nc.vector.tensor_copy(
-                    out=by_head[:].rearrange("p (hl jp d) -> p hl jp d", hl=HEADS_ROUND, jp=TOK_PASS)[:, heads],
-                    in_=x_raw[hh][:].rearrange("p jp (hl d) -> p hl jp d", d=DH)[:, heads],
-                )
-                bank = tpsum.tile([P, 512], F32, name="bank")
-                bank_out = bank[:].rearrange("p (u bg hlo thi) -> p u bg hlo thi", u=2, bg=BATCH * PASSES, hlo=2)
-                for hlo in range(2):
-                    for u in range(2):
-                        first = ((2 * q + hlo) * 2 + u) * P
-                        nc.tensor.transpose(
-                            bank_out[:, u, :, hlo, :], by_head_words[:, first : first + P], perm[:]
-                        )
-                nc.scalar.copy(
-                    out=grouped_words[:, q],
-                    in_=bank[:].rearrange("p (u bg m) -> p bg m u", u=2, bg=BATCH * PASSES),
-                )
-            for b in range(BATCH):
-                words = slice((hh * BATCH + b) * PASSES * P, (hh * BATCH + b + 1) * PASSES * P)
-                nc.vector.quantize_mx(
-                    out=y_codes[:, words].bitcast(FP8X4),
-                    scales=y_scales[:, words],
-                    in_=grouped[:, b * PASSES * P * 4 : (b + 1) * PASSES * P * 4],
-                )
+            return grouped
 
-        def multiply(hh, nh):
-            cols = slice(nh * N_HALF, (nh + 1) * N_HALF)
-            for b in range(BATCH):
-                acc = acc_psum.tile([P, N_HALF], F32, name="acc")
-                for g in range(PASSES):
-                    first = ((hh * BATCH + b) * PASSES + g) * P
-                    nc.tensor.matmul_mx(
-                        out=acc[:],
-                        lhsT=y_codes[:, first : first + P].bitcast(FP8X4),
-                        lhsT_scale=y_scales[:, first : first + P],
-                        rhs=w_codes[:, g, cols].bitcast(FP8X4),
-                        rhs_scale=w_scales[:, g, cols],
-                        start=(g == 0),
-                        stop=(g == PASSES - 1),
+        def quantise_w(nh, g, grouped):
+            nc.vector.quantize_mx(
+                out=w_codes[:, g, half(nh)].bitcast(FP8X4),
+                scales=w_scales[:, g, half(nh)],
+                in_=grouped[:].rearrange("p n t -> p (n t)"),
+            )
+
+        def sort_heads(r, q, copy):
+            heads = slice(BANK_HEADS * q, BANK_HEADS * (q + 1))
+            copy(
+                out=by_head[:, r].bitcast(F32).rearrange(
+                    "p (hl jp w) -> p hl jp w", hl=HEADS_ROUND, jp=TOK_PASS
+                )[:, heads],
+                in_=x_raw[:, r].bitcast(F32).rearrange("p jp (hl w) -> p hl jp w", w=DW)[:, heads],
+            )
+
+        def transpose_heads(r, q):
+            bank = psum.tile([P, N_HALF], F32, name="bank")
+            bank_out = bank[:].rearrange(
+                "p (u bg hlo thi) -> p u bg hlo thi", u=2, bg=BATCH * PASSES, hlo=BANK_HEADS
+            )
+            for hlo in range(BANK_HEADS):
+                for u in range(2):
+                    first = ((BANK_HEADS * q + hlo) * 2 + u) * P
+                    nc.tensor.transpose(
+                        bank_out[:, u, :, hlo, :],
+                        by_head[:, r].bitcast(F32)[:, first : first + P],
+                        perm[:],
                     )
-                result = results.tile([P, N_HALF], F32, name="result")
-                nc.vector.tensor_tensor(out=result[:], in0=acc[:], in1=bias[:, cols], op=mybir.AluOpType.add)
-                row = (b * HEAD_HALVES + hh) * P
-                nc.sync.dma_start(out=out_rows[row : row + P, cols], in_=result[:])
+            nc.scalar.copy(
+                out=y_grouped[:, r].bitcast(F32).rearrange(
+                    "p (bg q m u) -> p q bg m u", bg=BATCH * PASSES, q=BANKS_ROUND, u=2
+                )[:, q],
+                in_=bank[:].rearrange("p (u bg m) -> p bg m u", u=2, bg=BATCH * PASSES),
+            )
 
-        quantise_w(0)
-        quantise_y(0)
-        multiply(0, 0)
-        quantise_y(1)
-        multiply(1, 0)
-        quantise_w(1)
-        multiply(0, 1)
-        multiply(1, 1)
+        def quantise_y(r, b):
+            nc.vector.quantize_mx(
+                out=y_codes[:, r, b].bitcast(FP8X4),
+                scales=y_scales[:, r, b],
+                in_=y_grouped[:, r, b * TILE_WORDS * PACK : (b + 1) * TILE_WORDS * PACK],
+            )
+
+        def mx_pass(acc, r, nh, b, g, first):
+            nc.tensor.matmul_mx(
+                out=acc[:],
+                lhsT=y_codes[:, r, b, g * P : (g + 1) * P].bitcast(FP8X4),
+                lhsT_scale=y_scales[:, r, b, g * P : (g + 1) * P],
+                rhs=w_codes[:, g, half(nh)].bitcast(FP8X4),
+                rhs_scale=w_scales[:, g, half(nh)],
+                start=first,
+                stop=not first,
+            )
+
+        def finish(acc, r, nh, b):
+            result = results.tile([P, N_HALF], F32, name="result")
+            nc.vector.tensor_tensor(out=result[:], in0=acc[:], in1=bias[:, half(nh)], op=ADD)
+            row = (b * ROUNDS + r) * P
+            nc.sync.dma_start(out=out_rows[row : row + P, half(nh)], in_=result[:])
+
+        def multiply(r, nh, b):
+            acc = psum.tile([P, N_HALF], F32, name="bank")
+            mx_pass(acc, r, nh, b, 0, True)
+            mx_pass(acc, r, nh, b, 1, False)
+            finish(acc, r, nh, b)
+
+        for q in range(BANKS_ROUND):
+            sort_heads(0, q, nc.vector.tensor_copy)
+            transpose_heads(0, q)
+        spread_bias()
+        w00 = regroup_w(0, 0, nc.vector.tensor_copy)
+        w01 = regroup_w(0, 1, nc.vector.tensor_copy)
+        quantise_w(0, 0, w00)
+        quantise_w(0, 1, w01)
+        quantise_y(0, 0)
+        quantise_y(0, 1)
+        sort_heads(1, 0, nc.scalar.copy)
+        for i in range(BATCH):
+            if i + 1 < BANKS_ROUND:
+                sort_heads(1, i + 1, nc.scalar.copy)
+            multiply(0, 0, i)
+            if i + 2 < BATCH:
+                quantise_y(0, i + 2)
+            transpose_heads(1, i)
+        w10 = regroup_w(1, 0, nc.scalar.copy)
+        w11 = regroup_w(1, 1, nc.vector.tensor_copy)
+        quantise_y(1, 0)
+        quantise_y(1, 1)
+        quantise_w(1, 1, w11)
+        for b in range(BATCH):
+            multiply(1, 0, b)
+            if b + 2 < BATCH:
+                quantise_y(1, b + 2)
+        quantise_w(1, 0, w10)
+        tiles = [(r, b) for r in range(ROUNDS) for b in range(BATCH)]
+        open_banks = []
+        for r, b in tiles:
+            acc = psum.tile([P, N_HALF], F32, name="bank")
+            mx_pass(acc, r, 1, b, 1, True)
+            open_banks.append(acc)
+        for (r, b), acc in zip(tiles, open_banks):
+            mx_pass(acc, r, 1, b, 0, False)
+            finish(acc, r, 1, b)

@@ -78,9 +78,9 @@ def tile_reasoningmultiheadattention_pb_kernel(tc, h_attn, Wo, bo, out):
         nc.sync.dma_start(out=bias_row[0:1, :], in_=bo.unsqueeze(0))
         load_w(0, 0)
         load_w(0, 1)
-        load_x(1)
         load_w(1, 0)
         load_w(1, 1)
+        load_x(1)
 
         make_identity(nc, ident[:])
         nc.vector.tensor_copy(
@@ -94,7 +94,7 @@ def tile_reasoningmultiheadattention_pb_kernel(tc, h_attn, Wo, bo, out):
                 nc.tensor.matmul(
                     out=spread[:], lhsT=ones[:], rhs=bias_row[:, half(nh)], start=True, stop=True
                 )
-                nc.vector.tensor_copy(out=bias[:, half(nh)], in_=spread[:])
+                nc.scalar.copy(out=bias[:, half(nh)], in_=spread[:])
 
         def regroup_w(nh, g, copy):
             grouped = wstage.tile([P, N_HALF, PACK], BF16, align_bytes=64, name="w_grouped")
@@ -164,46 +164,43 @@ def tile_reasoningmultiheadattention_pb_kernel(tc, h_attn, Wo, bo, out):
             row = (b * ROUNDS + r) * P
             nc.sync.dma_start(out=out_rows[row : row + P, half(nh)], in_=result[:])
 
-        def multiply(r, nh, b):
-            acc = psum.tile([P, N_HALF], F32, name="bank")
-            mx_pass(acc, r, nh, b, 0, True)
-            mx_pass(acc, r, nh, b, 1, False)
-            finish(acc, r, nh, b)
+        def passes(r, nh):
+            banks = []
+            for b in range(BATCH):
+                acc = psum.tile([P, N_HALF], F32, name="bank")
+                mx_pass(acc, r, nh, b, 0, True)
+                mx_pass(acc, r, nh, b, 1, False)
+                banks.append(acc)
+            return banks
 
+        spread_bias()
         for q in range(BANKS_ROUND):
             sort_heads(0, q, nc.vector.tensor_copy)
             transpose_heads(0, q)
-        spread_bias()
         w00 = regroup_w(0, 0, nc.vector.tensor_copy)
         w01 = regroup_w(0, 1, nc.vector.tensor_copy)
         quantise_w(0, 0, w00)
         quantise_w(0, 1, w01)
-        quantise_y(0, 0)
-        quantise_y(0, 1)
-        sort_heads(1, 0, nc.scalar.copy)
-        for i in range(BATCH):
-            if i + 1 < BANKS_ROUND:
-                sort_heads(1, i + 1, nc.scalar.copy)
-            multiply(0, 0, i)
-            if i + 2 < BATCH:
-                quantise_y(0, i + 2)
-            transpose_heads(1, i)
         w10 = regroup_w(1, 0, nc.scalar.copy)
-        w11 = regroup_w(1, 1, nc.vector.tensor_copy)
-        quantise_y(1, 0)
-        quantise_y(1, 1)
-        quantise_w(1, 1, w11)
+        w11 = regroup_w(1, 1, nc.scalar.copy)
         for b in range(BATCH):
-            multiply(1, 0, b)
-            if b + 2 < BATCH:
-                quantise_y(1, b + 2)
+            quantise_y(0, b)
+        banks00 = passes(0, 0)
+        finish(banks00[0], 0, 0, 0)
+        finish(banks00[1], 0, 0, 1)
         quantise_w(1, 0, w10)
-        tiles = [(r, b) for r in range(ROUNDS) for b in range(BATCH)]
-        open_banks = []
-        for r, b in tiles:
-            acc = psum.tile([P, N_HALF], F32, name="bank")
-            mx_pass(acc, r, 1, b, 1, True)
-            open_banks.append(acc)
-        for (r, b), acc in zip(tiles, open_banks):
-            mx_pass(acc, r, 1, b, 0, False)
-            finish(acc, r, 1, b)
+        for q in range(BANKS_ROUND):
+            sort_heads(1, q, nc.vector.tensor_copy)
+            transpose_heads(1, q)
+        quantise_w(1, 1, w11)
+        finish(banks00[2], 0, 0, 2)
+        finish(banks00[3], 0, 0, 3)
+        banks01 = passes(0, 1)
+        for b in range(BATCH):
+            quantise_y(1, b)
+        for b in range(BATCH):
+            finish(banks01[b], 0, 1, b)
+        for nh in range(2):
+            banks1 = passes(1, nh)
+            for b in range(BATCH):
+                finish(banks1[b], 1, nh, b)

@@ -190,7 +190,8 @@ def tile_reasoningmultiheadattention_pb_kernel(tc, h_attn, Wo, bo, out):
         finish(banks00[1], 0, 0, 1)
         quantise_w(1, 0, w10)
         for q in range(BANKS_ROUND):
-            sort_heads(1, q, nc.vector.tensor_copy)
+            sort_heads(1, q, (nc.vector.tensor_copy, nc.scalar.copy)[q % 2])
+        for q in range(BANKS_ROUND):
             transpose_heads(1, q)
         quantise_w(1, 1, w11)
         finish(banks00[2], 0, 0, 2)

@@ -12,18 +12,25 @@ ADD = mybir.AluOpType.add
 
 P = 128
 BATCH, TOKENS, HEADS, DH = 4, 256, 16, 64
-K = HEADS * DH
+ROW_TOKENS = 16
+THI = TOKENS // ROW_TOKENS
+K = ROW_TOKENS * DH
 N = 1024
 PACK = 4
 PASSES = K // (PACK * P)
 N_HALF = 512
+N_HALVES = N // N_HALF
 ROUNDS = 2
-HEADS_ROUND = HEADS // ROUNDS
-TOK_PASS = 8
-DW = DH // 2
-BANK_HEADS = 2
-BANKS_ROUND = HEADS_ROUND // BANK_HEADS
+ROUND_BATCH = BATCH // ROUNDS
+JL = 4
+PAIRS = DH // 2
+BANK_HEADS = 4
+BANKS = HEADS // BANK_HEADS
+TILE_HEADS = P // THI
+HEAD_HALVES = HEADS // TILE_HEADS
+TILES = HEAD_HALVES * ROUND_BATCH
 TILE_WORDS = PASSES * P
+RUN = 4
 
 FLOPS = 2 * BATCH * TOKENS * K * N
 
@@ -33,13 +40,12 @@ def tile_reasoningmultiheadattention_pb_kernel(tc, h_attn, Wo, bo, out):
     with ExitStack() as stack:
         const = stack.enter_context(tc.tile_pool(name="const", bufs=1))
         keep = stack.enter_context(tc.tile_pool(name="keep", bufs=1))
-        wstage = stack.enter_context(tc.tile_pool(name="wstage", bufs=4))
         results = stack.enter_context(tc.tile_pool(name="results", bufs=8))
         psum = stack.enter_context(tc.psum_pool(name="psum", bufs=8))
         stack.enter_context(tc.manual_schedule())
 
         h_view = h_attn.rearrange(
-            "b (tg jp) (r hl) d -> (b tg) jp r (hl d)", jp=TOK_PASS, r=ROUNDS
+            "(r b) (t4 jl) h d -> r (b t4) (jl h d)", b=ROUND_BATCH, jl=JL
         )
         w_view = Wo.rearrange("(g u p e) n -> g u p e n", g=PASSES, u=2, e=2)
         out_rows = out.flatten_outer_dims()
@@ -50,17 +56,21 @@ def tile_reasoningmultiheadattention_pb_kernel(tc, h_attn, Wo, bo, out):
         ident = const.tile([P, P], F32)
         perm = const.tile([P, P], F32)
         bias = const.tile([P, N], F32)
-        w_raw = keep.tile([P, 2, PASSES, PACK, N_HALF], BF16)
-        x_raw = keep.tile([P, ROUNDS, TOK_PASS, HEADS_ROUND * DH], BF16)
-        by_head = keep.tile([P, ROUNDS, HEADS_ROUND * TOK_PASS * DH], BF16)
-        y_grouped = keep.tile([P, ROUNDS, BATCH * TILE_WORDS * PACK], BF16, align_bytes=64)
+        x_raw = keep.tile([P, ROUNDS, JL * HEADS * DH], BF16)
+        by_head = keep.tile([P, ROUNDS, HEADS * JL * DH], BF16)
+        y_grouped = keep.tile([P, ROUNDS, TILES * TILE_WORDS * PACK], BF16, align_bytes=64)
+        y_codes = keep.tile([P, ROUNDS, TILES, TILE_WORDS], U32, align_bytes=64)
+        y_scales = keep.tile([P, ROUNDS, TILES, TILE_WORDS], U8, align_bytes=64)
+        w_raw = keep.tile([P, N_HALVES, PASSES, PACK, N_HALF], BF16)
+        w_grouped = keep.tile([P, N_HALVES, PASSES, N_HALF * PACK], BF16, align_bytes=64)
         w_codes = keep.tile([P, PASSES, N], U32, align_bytes=64)
         w_scales = keep.tile([P, PASSES, N], U8, align_bytes=64)
-        y_codes = keep.tile([P, ROUNDS, BATCH, TILE_WORDS], U32, align_bytes=64)
-        y_scales = keep.tile([P, ROUNDS, BATCH, TILE_WORDS], U8, align_bytes=64)
 
         def half(nh):
             return slice(nh * N_HALF, (nh + 1) * N_HALF)
+
+        def load_x(r):
+            nc.sync.dma_start(out=x_raw[:, r], in_=h_view[r])
 
         def load_w(nh, g):
             for u in range(2):
@@ -68,28 +78,26 @@ def tile_reasoningmultiheadattention_pb_kernel(tc, h_attn, Wo, bo, out):
                     out=w_raw[:, nh, g, 2 * u : 2 * u + 2, :], in_=w_view[g, u][:, :, half(nh)]
                 )
 
-        def load_x(r):
-            nc.sync.dma_start(out=x_raw[:, r], in_=h_view[:, :, r, :])
-
         nc.vector.memset(bias_row[:], 0.0)
         nc.vector.memset(ones[:], 1.0)
         nc.scalar.copy(out=warm[:], in_=ones[:, 0:1])
         load_x(0)
         nc.sync.dma_start(out=bias_row[0:1, :], in_=bo.unsqueeze(0))
-        load_w(0, 0)
-        load_w(0, 1)
-        load_w(1, 0)
-        load_w(1, 1)
+        for nh in range(N_HALVES):
+            for g in range(PASSES):
+                load_w(nh, g)
         load_x(1)
 
         make_identity(nc, ident[:])
-        nc.vector.tensor_copy(
-            out=perm[:].rearrange("p (b g thi) -> p b g thi", b=BATCH, g=PASSES),
-            in_=ident[:].rearrange("p (b thi g) -> p b g thi", b=BATCH, g=PASSES),
-        )
+        for b in range(ROUND_BATCH):
+            cols = slice(b * P // ROUND_BATCH, (b + 1) * P // ROUND_BATCH)
+            nc.vector.tensor_copy(
+                out=perm[:, cols].rearrange("p (g thi u) -> p g thi u", g=PASSES, u=2),
+                in_=ident[:, cols].rearrange("p (thi g u) -> p g thi u", g=PASSES, u=2),
+            )
 
         def spread_bias():
-            for nh in range(2):
+            for nh in range(N_HALVES):
                 spread = psum.tile([P, N_HALF], F32, name="bank")
                 nc.tensor.matmul(
                     out=spread[:], lhsT=ones[:], rhs=bias_row[:, half(nh)], start=True, stop=True
@@ -97,111 +105,104 @@ def tile_reasoningmultiheadattention_pb_kernel(tc, h_attn, Wo, bo, out):
                 nc.scalar.copy(out=bias[:, half(nh)], in_=spread[:])
 
         def regroup_w(nh, g, copy):
-            grouped = wstage.tile([P, N_HALF, PACK], BF16, align_bytes=64, name="w_grouped")
             copy(
-                out=grouped[:].rearrange("p (c i) t -> p c t i", i=4),
-                in_=w_raw[:, nh, g].rearrange("p t (c i) -> p c t i", i=4),
+                out=w_grouped[:, nh, g].rearrange("p (c i t) -> p c t i", i=RUN, t=PACK),
+                in_=w_raw[:, nh, g].rearrange("p t (c i) -> p c t i", i=RUN),
             )
-            return grouped
 
-        def quantise_w(nh, g, grouped):
+        def quantise_w(nh, g):
             nc.vector.quantize_mx(
                 out=w_codes[:, g, half(nh)].bitcast(FP8X4),
                 scales=w_scales[:, g, half(nh)],
-                in_=grouped[:].rearrange("p n t -> p (n t)"),
+                in_=w_grouped[:, nh, g],
             )
 
-        def sort_heads(r, q, copy):
+        def sort_heads(r, q):
             heads = slice(BANK_HEADS * q, BANK_HEADS * (q + 1))
-            copy(
+            nc.vector.tensor_copy(
                 out=by_head[:, r].bitcast(F32).rearrange(
-                    "p (hl jp w) -> p hl jp w", hl=HEADS_ROUND, jp=TOK_PASS
+                    "p (h jl w) -> p h jl w", h=HEADS, jl=JL
                 )[:, heads],
-                in_=x_raw[:, r].bitcast(F32).rearrange("p jp (hl w) -> p hl jp w", w=DW)[:, heads],
+                in_=x_raw[:, r].bitcast(F32).rearrange(
+                    "p (jl h w) -> p h jl w", h=HEADS, jl=JL
+                )[:, heads],
             )
 
         def transpose_heads(r, q):
             bank = psum.tile([P, N_HALF], F32, name="bank")
-            bank_out = bank[:].rearrange(
-                "p (u bg hlo thi) -> p u bg hlo thi", u=2, bg=BATCH * PASSES, hlo=BANK_HEADS
-            )
-            for hlo in range(BANK_HEADS):
-                for u in range(2):
-                    first = ((BANK_HEADS * q + hlo) * 2 + u) * P
-                    nc.tensor.transpose(
-                        bank_out[:, u, :, hlo, :],
-                        by_head[:, r].bitcast(F32)[:, first : first + P],
-                        perm[:],
-                    )
+            for h4 in range(BANK_HEADS):
+                first = (BANK_HEADS * q + h4) * JL * PAIRS
+                nc.tensor.transpose(
+                    bank[:].rearrange("p (bg h tu) -> p bg h tu", h=BANK_HEADS, tu=THI * 2)[:, :, h4, :],
+                    by_head[:, r].bitcast(F32)[:, first : first + P],
+                    perm[:],
+                )
+            half_banks = BANKS // HEAD_HALVES
             nc.scalar.copy(
                 out=y_grouped[:, r].bitcast(F32).rearrange(
-                    "p (bg q m u) -> p q bg m u", bg=BATCH * PASSES, q=BANKS_ROUND, u=2
-                )[:, q],
-                in_=bank[:].rearrange("p (u bg m) -> p bg m u", u=2, bg=BATCH * PASSES),
+                    "p (hh bg part w) -> p hh part bg w", hh=HEAD_HALVES, part=half_banks, w=P
+                )[:, q // half_banks, q % half_banks],
+                in_=bank[:].rearrange("p (bg w) -> p bg w", w=P),
             )
 
-        def quantise_y(r, b):
+        def quantise_y(r, i):
             nc.vector.quantize_mx(
-                out=y_codes[:, r, b].bitcast(FP8X4),
-                scales=y_scales[:, r, b],
-                in_=y_grouped[:, r, b * TILE_WORDS * PACK : (b + 1) * TILE_WORDS * PACK],
+                out=y_codes[:, r, i].bitcast(FP8X4),
+                scales=y_scales[:, r, i],
+                in_=y_grouped[:, r, i * TILE_WORDS * PACK : (i + 1) * TILE_WORDS * PACK],
             )
 
-        def mx_pass(acc, r, nh, b, g, first):
-            nc.tensor.matmul_mx(
-                out=acc[:],
-                lhsT=y_codes[:, r, b, g * P : (g + 1) * P].bitcast(FP8X4),
-                lhsT_scale=y_scales[:, r, b, g * P : (g + 1) * P],
-                rhs=w_codes[:, g, half(nh)].bitcast(FP8X4),
-                rhs_scale=w_scales[:, g, half(nh)],
-                start=first,
-                stop=not first,
-            )
-
-        def finish(acc, r, nh, b):
-            result = results.tile([P, N_HALF], F32, name="result")
-            nc.vector.tensor_tensor(out=result[:], in0=acc[:], in1=bias[:, half(nh)], op=ADD)
-            row = (b * ROUNDS + r) * P
-            nc.sync.dma_start(out=out_rows[row : row + P, half(nh)], in_=result[:])
-
-        def passes(r, nh):
+        def multiply(r, nh):
             banks = []
-            for b in range(BATCH):
+            for i in range(TILES):
                 acc = psum.tile([P, N_HALF], F32, name="bank")
-                mx_pass(acc, r, nh, b, 0, True)
-                mx_pass(acc, r, nh, b, 1, False)
+                for g in range(PASSES):
+                    nc.tensor.matmul_mx(
+                        out=acc[:],
+                        lhsT=y_codes[:, r, i, g * P : (g + 1) * P].bitcast(FP8X4),
+                        lhsT_scale=y_scales[:, r, i, g * P : (g + 1) * P],
+                        rhs=w_codes[:, g, half(nh)].bitcast(FP8X4),
+                        rhs_scale=w_scales[:, g, half(nh)],
+                        start=(g == 0),
+                        stop=(g == PASSES - 1),
+                    )
                 banks.append(acc)
             return banks
 
+        def finish(acc, r, nh, i):
+            result = results.tile([P, N_HALF], F32, name="result")
+            nc.vector.tensor_tensor(out=result[:], in0=acc[:], in1=bias[:, half(nh)], op=ADD)
+            row = (ROUND_BATCH * r + i % ROUND_BATCH) * TOKENS + (i // ROUND_BATCH) * P
+            nc.sync.dma_start(out=out_rows[row : row + P, half(nh)], in_=result[:])
+
         spread_bias()
-        for q in range(BANKS_ROUND):
-            sort_heads(0, q, nc.vector.tensor_copy)
+        for q in range(BANKS):
+            sort_heads(0, q)
             transpose_heads(0, q)
-        w00 = regroup_w(0, 0, nc.vector.tensor_copy)
-        w01 = regroup_w(0, 1, nc.vector.tensor_copy)
-        quantise_w(0, 0, w00)
-        quantise_w(0, 1, w01)
-        w10 = regroup_w(1, 0, nc.scalar.copy)
-        w11 = regroup_w(1, 1, nc.scalar.copy)
-        for b in range(BATCH):
-            quantise_y(0, b)
-        banks00 = passes(0, 0)
-        finish(banks00[0], 0, 0, 0)
-        finish(banks00[1], 0, 0, 1)
-        quantise_w(1, 0, w10)
-        for q in range(BANKS_ROUND):
-            sort_heads(1, q, (nc.vector.tensor_copy, nc.scalar.copy)[q % 2])
-        for q in range(BANKS_ROUND):
+        for g in range(PASSES):
+            regroup_w(0, g, nc.vector.tensor_copy)
+        for g in range(PASSES):
+            quantise_w(0, g)
+        for g in range(PASSES):
+            regroup_w(1, g, nc.scalar.copy)
+        for i in range(TILES):
+            quantise_y(0, i)
+        first_banks = multiply(0, 0)
+        for i in range(TILES // 2):
+            finish(first_banks[i], 0, 0, i)
+        quantise_w(1, 0)
+        for q in range(BANKS):
+            sort_heads(1, q)
             transpose_heads(1, q)
-        quantise_w(1, 1, w11)
-        finish(banks00[2], 0, 0, 2)
-        finish(banks00[3], 0, 0, 3)
-        banks01 = passes(0, 1)
-        for b in range(BATCH):
-            quantise_y(1, b)
-        for b in range(BATCH):
-            finish(banks01[b], 0, 1, b)
-        for nh in range(2):
-            banks1 = passes(1, nh)
-            for b in range(BATCH):
-                finish(banks1[b], 1, nh, b)
+        quantise_w(1, 1)
+        for i in range(TILES // 2, TILES):
+            finish(first_banks[i], 0, 0, i)
+        second_banks = multiply(0, 1)
+        for i in range(TILES):
+            quantise_y(1, i)
+        for i in range(TILES):
+            finish(second_banks[i], 0, 1, i)
+        for nh in range(N_HALVES):
+            banks = multiply(1, nh)
+            for i in range(TILES):
+                finish(banks[i], 1, nh, i)

@@ -169,11 +169,22 @@ def tile_reasoningmultiheadattention_pb_kernel(tc, h_attn, Wo, bo, out):
                 banks.append(acc)
             return banks
 
+        def store(result, r, nh, i):
+            row = (ROUND_BATCH * r + i % ROUND_BATCH) * TOKENS + (i // ROUND_BATCH) * P
+            nc.sync.dma_start(out=out_rows[row : row + P, half(nh)], in_=result[:])
+
         def finish(acc, r, nh, i):
             result = results.tile([P, N_HALF], F32, name="result")
             nc.vector.tensor_tensor(out=result[:], in0=acc[:], in1=bias[:, half(nh)], op=ADD)
-            row = (ROUND_BATCH * r + i % ROUND_BATCH) * TOKENS + (i // ROUND_BATCH) * P
-            nc.sync.dma_start(out=out_rows[row : row + P, half(nh)], in_=result[:])
+            store(result, r, nh, i)
+
+        def finish_group(banks, r, nh):
+            side = results.tile([P, N_HALF], F32, name="result")
+            nc.scalar.copy(out=side[:], in_=banks[0][:])
+            nc.gpsimd.tensor_tensor(out=side[:], in0=side[:], in1=bias[:, half(nh)], op=ADD)
+            for i in range(1, TILES):
+                finish(banks[i], r, nh, i)
+            store(side, r, nh, 0)
 
         spread_bias()
         for q in range(BANKS):
@@ -200,9 +211,6 @@ def tile_reasoningmultiheadattention_pb_kernel(tc, h_attn, Wo, bo, out):
         second_banks = multiply(0, 1)
         for i in range(TILES):
             quantise_y(1, i)
-        for i in range(TILES):
-            finish(second_banks[i], 0, 1, i)
+        finish_group(second_banks, 0, 1)
         for nh in range(N_HALVES):
-            banks = multiply(1, nh)
-            for i in range(TILES):
-                finish(banks[i], 1, nh, i)
+            finish_group(multiply(1, nh), 1, nh)

from contextlib import ExitStack

from concourse import mybir
from concourse.masks import make_identity

BF16 = mybir.dt.bfloat16
F32 = mybir.dt.float32
U32 = mybir.dt.uint32
U8 = mybir.dt.uint8
FP8X4 = mybir.dt.float8_e4m3fn_x4
ADD = mybir.AluOpType.add

P = 128
BATCH, TOKENS, HEADS, DH = 4, 256, 16, 64
ROW_TOKENS = 16
THI = TOKENS // ROW_TOKENS
K = ROW_TOKENS * DH
N = 1024
PACK = 4
PASSES = K // (PACK * P)
N_HALF = 512
N_HALVES = N // N_HALF
ROUNDS = 2
ROUND_BATCH = BATCH // ROUNDS
JL = 4
PAIRS = DH // 2
BANK_HEADS = 4
BANKS = HEADS // BANK_HEADS
TILE_HEADS = P // THI
HEAD_HALVES = HEADS // TILE_HEADS
TILES = HEAD_HALVES * ROUND_BATCH
TILE_WORDS = PASSES * P
RUN = 4

FLOPS = 2 * BATCH * TOKENS * K * N


def tile_reasoningmultiheadattention_pb_kernel(tc, h_attn, Wo, bo, out):
    nc = tc.nc
    with ExitStack() as stack:
        const = stack.enter_context(tc.tile_pool(name="const", bufs=1))
        keep = stack.enter_context(tc.tile_pool(name="keep", bufs=1))
        results = stack.enter_context(tc.tile_pool(name="results", bufs=8))
        psum = stack.enter_context(tc.psum_pool(name="psum", bufs=8))
        stack.enter_context(tc.manual_schedule())

        h_view = h_attn.rearrange(
            "(r b) (t4 jl) h d -> r (b t4) (jl h d)", b=ROUND_BATCH, jl=JL
        )
        w_view = Wo.rearrange("(g u p e) n -> g u p e n", g=PASSES, u=2, e=2)
        out_rows = out.flatten_outer_dims()

        bias_row = const.tile([P, N], BF16)
        ones = const.tile([P, P], BF16)
        warm = const.tile([P, 1], BF16)
        ident = const.tile([P, P], F32)
        perm = const.tile([P, P], F32)
        bias = const.tile([P, N], F32)
        x_raw = keep.tile([P, ROUNDS, JL * HEADS * DH], BF16)
        by_head = keep.tile([P, ROUNDS, HEADS * JL * DH], BF16)
        y_grouped = keep.tile([P, ROUNDS, TILES * TILE_WORDS * PACK], BF16, align_bytes=64)
        y_codes = keep.tile([P, ROUNDS, TILES, TILE_WORDS], U32, align_bytes=64)
        y_scales = keep.tile([P, ROUNDS, TILES, TILE_WORDS], U8, align_bytes=64)
        w_raw = keep.tile([P, N_HALVES, PASSES, PACK, N_HALF], BF16)
        w_grouped = keep.tile([P, N_HALVES, PASSES, N_HALF * PACK], BF16, align_bytes=64)
        w_codes = keep.tile([P, PASSES, N], U32, align_bytes=64)
        w_scales = keep.tile([P, PASSES, N], U8, align_bytes=64)

        def half(nh):
            return slice(nh * N_HALF, (nh + 1) * N_HALF)

        def load_x(r):
            nc.sync.dma_start(out=x_raw[:, r], in_=h_view[r])

        def load_w(nh, g):
            for u in range(2):
                nc.sync.dma_start(
                    out=w_raw[:, nh, g, 2 * u : 2 * u + 2, :], in_=w_view[g, u][:, :, half(nh)]
                )

        nc.vector.memset(bias_row[:], 0.0)
        nc.vector.memset(ones[:], 1.0)
        nc.scalar.copy(out=warm[:], in_=ones[:, 0:1])
        load_x(0)
        nc.sync.dma_start(out=bias_row[0:1, :], in_=bo.unsqueeze(0))
        for nh in range(N_HALVES):
            for g in range(PASSES):
                load_w(nh, g)
        load_x(1)

        make_identity(nc, ident[:])
        for b in range(ROUND_BATCH):
            cols = slice(b * P // ROUND_BATCH, (b + 1) * P // ROUND_BATCH)
            nc.vector.tensor_copy(
                out=perm[:, cols].rearrange("p (g thi u) -> p g thi u", g=PASSES, u=2),
                in_=ident[:, cols].rearrange("p (thi g u) -> p g thi u", g=PASSES, u=2),
            )

        def spread_bias():
            for nh in range(N_HALVES):
                spread = psum.tile([P, N_HALF], F32, name="bank")
                nc.tensor.matmul(
                    out=spread[:], lhsT=ones[:], rhs=bias_row[:, half(nh)], start=True, stop=True
                )
                nc.scalar.copy(out=bias[:, half(nh)], in_=spread[:])

        def regroup_w(nh, g, copy):
            copy(
                out=w_grouped[:, nh, g].rearrange("p (c i t) -> p c t i", i=RUN, t=PACK),
                in_=w_raw[:, nh, g].rearrange("p t (c i) -> p c t i", i=RUN),
            )

        def quantise_w(nh, g):
            nc.vector.quantize_mx(
                out=w_codes[:, g, half(nh)].bitcast(FP8X4),
                scales=w_scales[:, g, half(nh)],
                in_=w_grouped[:, nh, g],
            )

        def sort_heads(r, q):
            heads = slice(BANK_HEADS * q, BANK_HEADS * (q + 1))
            nc.vector.tensor_copy(
                out=by_head[:, r].bitcast(F32).rearrange(
                    "p (h jl w) -> p h jl w", h=HEADS, jl=JL
                )[:, heads],
                in_=x_raw[:, r].bitcast(F32).rearrange(
                    "p (jl h w) -> p h jl w", h=HEADS, jl=JL
                )[:, heads],
            )

        def transpose_heads(r, q):
            bank = psum.tile([P, N_HALF], F32, name="bank")
            for h4 in range(BANK_HEADS):
                first = (BANK_HEADS * q + h4) * JL * PAIRS
                nc.tensor.transpose(
                    bank[:].rearrange("p (bg h tu) -> p bg h tu", h=BANK_HEADS, tu=THI * 2)[:, :, h4, :],
                    by_head[:, r].bitcast(F32)[:, first : first + P],
                    perm[:],
                )
            half_banks = BANKS // HEAD_HALVES
            nc.scalar.copy(
                out=y_grouped[:, r].bitcast(F32).rearrange(
                    "p (hh bg part w) -> p hh part bg w", hh=HEAD_HALVES, part=half_banks, w=P
                )[:, q // half_banks, q % half_banks],
                in_=bank[:].rearrange("p (bg w) -> p bg w", w=P),
            )

        def quantise_y(r, i):
            nc.vector.quantize_mx(
                out=y_codes[:, r, i].bitcast(FP8X4),
                scales=y_scales[:, r, i],
                in_=y_grouped[:, r, i * TILE_WORDS * PACK : (i + 1) * TILE_WORDS * PACK],
            )

        def multiply(r, nh):
            banks = []
            for i in range(TILES):
                acc = psum.tile([P, N_HALF], F32, name="bank")
                for g in range(PASSES):
                    nc.tensor.matmul_mx(
                        out=acc[:],
                        lhsT=y_codes[:, r, i, g * P : (g + 1) * P].bitcast(FP8X4),
                        lhsT_scale=y_scales[:, r, i, g * P : (g + 1) * P],
                        rhs=w_codes[:, g, half(nh)].bitcast(FP8X4),
                        rhs_scale=w_scales[:, g, half(nh)],
                        start=(g == 0),
                        stop=(g == PASSES - 1),
                    )
                banks.append(acc)
            return banks

        def store(result, r, nh, i):
            row = (ROUND_BATCH * r + i % ROUND_BATCH) * TOKENS + (i // ROUND_BATCH) * P
            nc.sync.dma_start(out=out_rows[row : row + P, half(nh)], in_=result[:])

        def finish(acc, r, nh, i):
            result = results.tile([P, N_HALF], F32, name="result")
            nc.vector.tensor_tensor(out=result[:], in0=acc[:], in1=bias[:, half(nh)], op=ADD)
            store(result, r, nh, i)

        def finish_group(banks, r, nh):
            side = results.tile([P, N_HALF], F32, name="result")
            nc.scalar.copy(out=side[:], in_=banks[0][:])
            nc.gpsimd.tensor_tensor(out=side[:], in0=side[:], in1=bias[:, half(nh)], op=ADD)
            for i in range(1, TILES):
                finish(banks[i], r, nh, i)
            store(side, r, nh, 0)

        spread_bias()
        for q in range(BANKS):
            sort_heads(0, q)
            transpose_heads(0, q)
        for g in range(PASSES):
            regroup_w(0, g, nc.vector.tensor_copy)
        for g in range(PASSES):
            quantise_w(0, g)
        for g in range(PASSES):
            regroup_w(1, g, nc.scalar.copy)
        for i in range(TILES):
            quantise_y(0, i)
        first_banks = multiply(0, 0)
        for i in range(TILES // 2):
            finish(first_banks[i], 0, 0, i)
        quantise_w(1, 0)
        for q in range(BANKS):
            sort_heads(1, q)
            transpose_heads(1, q)
        quantise_w(1, 1)
        for i in range(TILES // 2, TILES):
            finish(first_banks[i], 0, 0, i)
        second_banks = multiply(0, 1)
        for i in range(TILES):
            quantise_y(1, i)
        finish_group(second_banks, 0, 1)
        for nh in range(N_HALVES):
            finish_group(multiply(1, nh), 1, nh)
